import numpy as np
import ml_dtypes


def mxq(x, axis, fmt="e4m3"):
    dtype, down = {"e4m3": (ml_dtypes.float8_e4m3fn, 7), "e5m2": (ml_dtypes.float8_e5m2, 14)}[fmt]
    v = np.moveaxis(np.asarray(x, np.float32).astype(ml_dtypes.bfloat16).astype(np.float64), axis, -1)
    blocks = v.reshape(v.shape[:-1] + (-1, 32))
    amax = np.abs(blocks).max(-1, keepdims=True)
    byte = np.maximum(np.where(amax > 0, np.frexp(amax)[1] - 1 + 127, 0) - down, 1)
    scale = np.exp2(byte - 127.0)
    codes = (blocks / scale).astype(np.float32).astype(dtype).astype(np.float64)
    return np.moveaxis((codes * scale).reshape(v.shape), -1, axis)


WIDE = False


def mx_kscale(k):
    if not WIDE:
        return np.ones(k)
    levels = np.array([10, -10, 5, -5, 0])
    a = np.random.permutation(np.resize(levels, k // 512 * 4)).reshape(k // 512, 4)
    idx = np.arange(k)
    return np.exp2(a[idx // 512, idx % 128 // 32])


BF16 = ml_dtypes.bfloat16


def bf(x):
    return np.asarray(x, np.float32).astype(BF16)


def f64(x):
    return np.asarray(x).astype(np.float64)


B, S, C, HD = 4, 1024, 1024, 128
H = C // HD
HP = HD // 2
EPS = 1e-6
THETA = 10000.0


def rmsnorm(h, g):
    return h * (1.0 / np.sqrt(np.mean(h * h, axis=-1, keepdims=True) + EPS)) * g


def apply_rope1(h, freqs):
    sh = h.shape
    h_ = h.reshape(*sh[:-1], -1, 1, 2)
    out = freqs[..., 0] * h_[..., 0] + freqs[..., 1] * h_[..., 1]
    return out.reshape(sh)


def setup_inputs():
    s = mx_kscale(C)
    pos = f64(np.random.randint(0, S, size=(S, 1)))
    inv_freq = 1.0 / THETA ** (np.arange(HP) / HP)
    ang = pos * inv_freq
    cos, sin = np.cos(ang), np.sin(ang)
    rot = np.stack([np.stack([cos, -sin], -1), np.stack([sin, cos], -1)], -2)
    return {"x": bf(np.random.standard_normal((B, S, C)) * s),
            "freqs": bf(rot[None, :, None]),
            "w": bf(np.random.standard_normal((C, C)) / np.sqrt(C) / s[None, :]),
            "b": bf(np.random.standard_normal(C) * 0.3),
            "g": bf(1.0 + 0.1 * np.random.standard_normal(HD))}


def reference(x, freqs, w, b, g):
    p = (mxq(f64(x), 2, "e4m3") @ mxq(f64(w), 1, "e4m3").T) + f64(b)
    h = p.reshape(B, S, H, HD)
    return apply_rope1(rmsnorm(h, f64(g)), f64(freqs))

@@ -1,0 +1,255 @@
+from contextlib import ExitStack
+
+import concourse.mybir as mybir
+from concourse.masks import make_identity
+
+F32 = mybir.dt.float32
+BF16 = mybir.dt.bfloat16
+U32 = mybir.dt.uint32
+U8 = mybir.dt.uint8
+FP8X4 = mybir.dt.float8_e4m3fn_x4
+ACT = mybir.ActivationFunctionType
+ALU = mybir.AluOpType
+
+P = 128
+K = 1024
+K_PASSES = 2
+WORDS_PER_PASS = 256
+HEADS = 8
+HEAD_DIM = 128
+PAIRS = HEAD_DIM // 2
+EPS = 1e-6
+TOKENS = 4096
+GROUP = 512
+GROUPS = TOKENS // GROUP
+TILES = GROUP // P
+ALL_TILES = GROUPS * TILES
+SEQ_HALVES = 2
+BLOCK_ROWS = 256
+X_BLOCKS = GROUPS * (GROUP // BLOCK_ROWS) * K_PASSES
+W_CHUNKS = HEADS * HEAD_DIM // BLOCK_ROWS
+BANK_HEADS = 4
+PROJECT_AHEAD = TILES
+QUANTISE_AHEAD = 2 * TILES
+
+FLOPS = 2 * TOKENS * K * HEADS * HEAD_DIM
+
+
+def tile_selfattention_pa_t_kernel(tc, x, freqs, w, b, g, out):
+    nc = tc.nc
+    x_groups = x.rearrange("n s k -> (n s) k").rearrange("(a q t) k -> a q t k", q=P, t=TILES)
+    out_tiles = out.rearrange("n s h d -> (n s) (h d)").rearrange("(a q t) f -> a t q f", q=P, t=TILES)
+    w_chunks = w.rearrange("(c r q) k -> c q r k", r=2, q=P)
+    freqs_rows = freqs.rearrange("a s b j r i -> (a s b) (j r i)").rearrange(
+        "(e q t) f -> q e t f", q=P, t=TILES
+    )
+
+    with ExitStack() as ctx:
+        keep = ctx.enter_context(tc.tile_pool(name="keep", bufs=1))
+        grouped_pool = ctx.enter_context(tc.tile_pool(name="grouped_pool", bufs=3))
+        x_mx_pool = ctx.enter_context(tc.tile_pool(name="x_mx_pool", bufs=3))
+        biased_pool = ctx.enter_context(tc.tile_pool(name="biased_pool", bufs=2 * HEADS))
+        small_pool = ctx.enter_context(tc.tile_pool(name="small_pool", bufs=4))
+        prod_pool = ctx.enter_context(tc.tile_pool(name="prod_pool", bufs=4))
+        result_pool = ctx.enter_context(tc.tile_pool(name="result_pool", bufs=3))
+        words_psum = ctx.enter_context(tc.psum_pool(name="words_psum", bufs=2))
+        acc_psum = ctx.enter_context(tc.psum_pool(name="acc_psum", bufs=2))
+        u_psum = ctx.enter_context(tc.psum_pool(name="u_psum", bufs=4))
+        ctx.enter_context(tc.manual_schedule())
+
+        x_sb = keep.tile([P, GROUPS, TILES, K], BF16, name="x_sb")
+        w_sb = keep.tile([P, HEADS, K], BF16, name="w_sb")
+        b_rows_bf = keep.tile([HEADS, HEAD_DIM], BF16, name="b_rows_bf")
+        g_all = keep.tile([P, HEAD_DIM], BF16, name="g_all")
+        freqs_sb = keep.tile([P, SEQ_HALVES, TILES, 4 * PAIRS], BF16, name="freqs_sb")
+        nc.sync.dma_start(out=x_sb[:, 0], in_=x_groups[0])
+        nc.sync.dma_start(out=b_rows_bf[:], in_=b.rearrange("(h d) -> h d", d=HEAD_DIM))
+        nc.sync.dma_start(out=w_sb[:, 0:2, :], in_=w_chunks[0])
+        nc.sync.dma_start(out=x_sb[:, 1], in_=x_groups[1])
+        for c in range(1, W_CHUNKS):
+            nc.sync.dma_start(out=w_sb[:, 2 * c : 2 * c + 2, :], in_=w_chunks[c])
+        nc.sync.dma_start(out=g_all[:], in_=g.partition_broadcast(P))
+        nc.sync.dma_start(out=freqs_sb[:], in_=freqs_rows)
+        for a in range(2, GROUPS):
+            nc.sync.dma_start(out=x_sb[:, a], in_=x_groups[a])
+
+        ident = keep.tile([P, P], F32, name="ident")
+        make_identity(nc, ident[:])
+
+        def transpose_block(rows, k_pass):
+            words = words_psum.tile([P, 2, BLOCK_ROWS], F32, name="words")
+            for u in range(2):
+                first = WORDS_PER_PASS * k_pass + P * u
+                for r in range(2):
+                    nc.tensor.transpose(
+                        words[:, u, P * r : P * (r + 1)],
+                        rows[:, r, :].bitcast(F32)[:, first : first + P],
+                        ident[:],
+                    )
+            grouped = grouped_pool.tile([P, 4 * BLOCK_ROWS], BF16, name="grouped", align_bytes=64)
+            copy_out = nc.scalar.copy if k_pass == 0 else nc.vector.tensor_copy
+            copy_out(
+                out=grouped[:].bitcast(F32).rearrange("q (n u) -> q n u", u=2),
+                in_=words[:].rearrange("q u n -> q n u"),
+            )
+            return grouped
+
+        def quantise_block(grouped, codes, scales):
+            nc.vector.quantize_mx(out=codes.bitcast(FP8X4), scales=scales, in_=grouped[:])
+
+        x_codes = {}
+        x_scales = {}
+
+        def transpose_x_block(block):
+            group, rest = divmod(block, X_BLOCKS // GROUPS)
+            half, k_pass = divmod(rest, K_PASSES)
+            if rest == 0:
+                x_codes[group] = x_mx_pool.tile([P, K_PASSES, GROUP], U32, name="x_codes", align_bytes=64)
+                x_scales[group] = x_mx_pool.tile([P, K_PASSES, GROUP], U8, name="x_scales", align_bytes=64)
+            return transpose_block(x_sb[:, group, 2 * half : 2 * half + 2, :], k_pass)
+
+        def quantise_x_block(block, grouped):
+            group, rest = divmod(block, X_BLOCKS // GROUPS)
+            half, k_pass = divmod(rest, K_PASSES)
+            cols = slice(BLOCK_ROWS * half, BLOCK_ROWS * (half + 1))
+            quantise_block(grouped, x_codes[group][:, k_pass, cols], x_scales[group][:, k_pass, cols])
+
+        w_codes = keep.tile([P, K_PASSES, HEADS * HEAD_DIM], U32, name="w_codes", align_bytes=64)
+        w_scales = keep.tile([P, K_PASSES, HEADS * HEAD_DIM], U8, name="w_scales", align_bytes=64)
+
+        def quantise_w_chunk(c):
+            cols = slice(BLOCK_ROWS * c, BLOCK_ROWS * (c + 1))
+            for k_pass in range(K_PASSES):
+                grouped = transpose_block(w_sb[:, 2 * c : 2 * c + 2, :], k_pass)
+                quantise_block(grouped, w_codes[:, k_pass, cols], w_scales[:, k_pass, cols])
+
+        for block in range(QUANTISE_AHEAD - PROJECT_AHEAD):
+            quantise_x_block(block, transpose_x_block(block))
+
+        b_rows = keep.tile([P, P], F32, name="b_rows")
+        nc.vector.memset(b_rows[:], 0.0)
+        nc.vector.tensor_copy(out=b_rows[0:HEADS, :], in_=b_rows_bf[:])
+        b_turned = words_psum.tile([P, 2, BLOCK_ROWS], F32, name="words")
+        nc.tensor.transpose(b_turned[:, 0, 0:P], b_rows[:], ident[:])
+        b_col = keep.tile([P, HEADS], F32, name="b_col")
+        nc.vector.tensor_copy(out=b_col[:], in_=b_turned[:, 0, 0:HEADS])
+
+        matrices = keep.tile([P, SEQ_HALVES, TILES, 2, HEAD_DIM], F32, name="matrices")
+
+        def build_matrices(e, t):
+            nc.vector.tensor_tensor(
+                out=matrices[:, e, t].rearrange("q r (j i) -> q r j i", i=2),
+                in0=freqs_sb[:, e, t, :].rearrange("q (j r i) -> q r j i", r=2, i=2),
+                in1=g_all[:].rearrange("q (j i) -> q j i", i=2).unsqueeze(1).to_broadcast([P, 2, PAIRS, 2]),
+                op=ALU.mult,
+            )
+
+        biased = {}
+
+        def project(group, head):
+            acc = acc_psum.tile([P, GROUP], F32, name="acc")
+            feats = slice(HEAD_DIM * head, HEAD_DIM * (head + 1))
+            for k_pass in range(K_PASSES):
+                nc.tensor.matmul_mx(
+                    out=acc[:],
+                    lhsT=w_codes[:, k_pass, feats].bitcast(FP8X4),
+                    lhsT_scale=w_scales[:, k_pass, feats],
+                    rhs=x_codes[group][:, k_pass, :].bitcast(FP8X4),
+                    rhs_scale=x_scales[group][:, k_pass, :],
+                    start=(k_pass == 0),
+                    stop=(k_pass == K_PASSES - 1),
+                )
+            return acc
+
+        def add_bias(acc, group, head):
+            biased[group, head] = biased_pool.tile([P, GROUP], F32, name="biased")
+            nc.scalar.activation(
+                out=biased[group, head][:], in_=acc[:], func=ACT.Identity, bias=b_col[:, head : head + 1], scale=1.0
+            )
+
+        def turn_back(group, t, bank):
+            u = u_psum.tile([P, BANK_HEADS, HEAD_DIM], F32, name="u")
+            for h in range(BANK_HEADS):
+                nc.tensor.transpose(
+                    u[:, h, :], biased[group, BANK_HEADS * bank + h][:, P * t : P * (t + 1)], ident[:]
+                )
+            return u
+
+        def sum_squares(u):
+            sums = small_pool.tile([P, BANK_HEADS], F32, name="sums")
+            squares = small_pool.tile([P, BANK_HEADS, HEAD_DIM], F32, name="squares")
+            for h in range(BANK_HEADS):
+                nc.scalar.activation(
+                    out=squares[:, h, :], in_=u[:, h, :], func=ACT.Square, accum_out=sums[:, h : h + 1]
+                )
+            return sums
+
+        def inverse_rms(sums):
+            rstd = small_pool.tile([P, BANK_HEADS], F32, name="rstd")
+            nc.scalar.activation(
+                out=rstd[:], in_=sums[:], func=ACT.Abs_reciprocal_sqrt, scale=1.0 / HEAD_DIM, bias=EPS
+            )
+            return rstd
+
+        def multiply(u, rstd, matrix):
+            prod = prod_pool.tile([P, 2, BANK_HEADS, HEAD_DIM], F32, name="prod")
+            for h in range(BANK_HEADS):
+                nc.vector.scalar_tensor_tensor(
+                    out=prod[:, :, h, :],
+                    in0=u[:, h, :].unsqueeze(1).to_broadcast([P, 2, HEAD_DIM]),
+                    scalar=rstd[:, h : h + 1],
+                    in1=matrix,
+                    op0=ALU.mult,
+                    op1=ALU.mult,
+                )
+            return prod
+
+        def add_pairs(prod, result_half):
+            terms = prod[:].rearrange("q r h (j i) -> q i h j r", i=2)
+            nc.gpsimd.tensor_tensor(
+                out=result_half.rearrange("q (h j r) -> q h j r", h=BANK_HEADS, r=2),
+                in0=terms[:, 0],
+                in1=terms[:, 1],
+                op=ALU.add,
+            )
+
+        bank_cols = BANK_HEADS * HEAD_DIM
+        for i in range(-PROJECT_AHEAD, ALL_TILES):
+            ahead_group, head_pair = divmod(i + PROJECT_AHEAD, TILES)
+            projecting = ahead_group < GROUPS
+            finishing = i >= 0
+            block = i + QUANTISE_AHEAD
+            group, t = divmod(i, TILES)
+
+            if finishing:
+                u_0 = turn_back(group, t, 0)
+                u_1 = turn_back(group, t, 1)
+            else:
+                quantise_w_chunk(head_pair)
+            if projecting:
+                acc_0 = project(ahead_group, 2 * head_pair)
+                acc_1 = project(ahead_group, 2 * head_pair + 1)
+            if finishing:
+                sums_0 = sum_squares(u_0)
+            if projecting:
+                add_bias(acc_0, ahead_group, 2 * head_pair)
+            if finishing:
+                rstd_0 = inverse_rms(sums_0)
+            if projecting:
+                add_bias(acc_1, ahead_group, 2 * head_pair + 1)
+            if finishing:
+                sums_1 = sum_squares(u_1)
+            if block < X_BLOCKS:
+                grouped = transpose_x_block(block)
+            if finishing:
+                rstd_1 = inverse_rms(sums_1)
+                if group < SEQ_HALVES:
+                    build_matrices(group, t)
+                matrix = matrices[:, group % SEQ_HALVES, t]
+                result = result_pool.tile([P, HEADS * HEAD_DIM], F32, name="result")
+                add_pairs(multiply(u_0, rstd_0, matrix), result[:, 0:bank_cols])
+            if block < X_BLOCKS:
+                quantise_x_block(block, grouped)
+            if finishing:
+                add_pairs(multiply(u_1, rstd_1, matrix), result[:, bank_cols : 2 * bank_cols])
+                nc.sync.dma_start(out=out_tiles[group, t], in_=result[:])

@@ -75,6 +75,10 @@ def tile_selfattention_pa_t_kernel(tc, x, freqs, w, b, g, out):
 
         ident = keep.tile([P, P], F32, name="ident")
         make_identity(nc, ident[:])
+        sort_pairs = keep.tile([P, P], F32, name="sort_pairs")
+        nc.vector.tensor_copy(
+            out=sort_pairs[:].rearrange("q (i j) -> q i j", i=2), in_=ident[:].rearrange("q (j i) -> q i j", i=2)
+        )
 
         def transpose_block(rows, k_pass):
             words = words_psum.tile([P, 2, BLOCK_ROWS], F32, name="words")
@@ -134,13 +138,13 @@ def tile_selfattention_pa_t_kernel(tc, x, freqs, w, b, g, out):
         b_col = keep.tile([P, HEADS], F32, name="b_col")
         nc.vector.tensor_copy(out=b_col[:], in_=b_turned[:, 0, 0:HEADS])
 
-        matrices = keep.tile([P, SEQ_HALVES, TILES, 2, HEAD_DIM], F32, name="matrices")
+        matrices = keep.tile([P, SEQ_HALVES, TILES, 2, PAIRS, 2], F32, name="matrices")
 
         def build_matrices(e, t):
             nc.vector.tensor_tensor(
-                out=matrices[:, e, t].rearrange("q r (j i) -> q r j i", i=2),
-                in0=freqs_sb[:, e, t, :].rearrange("q (j r i) -> q r j i", r=2, i=2),
-                in1=g_all[:].rearrange("q (j i) -> q j i", i=2).unsqueeze(1).to_broadcast([P, 2, PAIRS, 2]),
+                out=matrices[:, e, t],
+                in0=freqs_sb[:, e, t, :].rearrange("q (j r i) -> q i j r", r=2, i=2),
+                in1=g_all[:].rearrange("q (j i) -> q i j", i=2).unsqueeze(3).to_broadcast([P, 2, PAIRS, 2]),
                 op=ALU.mult,
             )
 
@@ -171,7 +175,7 @@ def tile_selfattention_pa_t_kernel(tc, x, freqs, w, b, g, out):
             u = u_psum.tile([P, BANK_HEADS, HEAD_DIM], F32, name="u")
             for h in range(BANK_HEADS):
                 nc.tensor.transpose(
-                    u[:, h, :], biased[group, BANK_HEADS * bank + h][:, P * t : P * (t + 1)], ident[:]
+                    u[:, h, :], biased[group, BANK_HEADS * bank + h][:, P * t : P * (t + 1)], sort_pairs[:]
                 )
             return u
 
@@ -192,24 +196,23 @@ def tile_selfattention_pa_t_kernel(tc, x, freqs, w, b, g, out):
             return rstd
 
         def multiply(u, rstd, matrix):
-            prod = prod_pool.tile([P, 2, BANK_HEADS, HEAD_DIM], F32, name="prod")
+            prod = prod_pool.tile([P, BANK_HEADS, 2, HEAD_DIM], F32, name="prod")
             for h in range(BANK_HEADS):
                 nc.vector.scalar_tensor_tensor(
-                    out=prod[:, :, h, :],
-                    in0=u[:, h, :].unsqueeze(1).to_broadcast([P, 2, HEAD_DIM]),
+                    out=prod[:, h].rearrange("q i (j r) -> q (i j) r", r=2),
+                    in0=u[:, h, :].unsqueeze(2).to_broadcast([P, HEAD_DIM, 2]),
                     scalar=rstd[:, h : h + 1],
-                    in1=matrix,
+                    in1=matrix.rearrange("q i j r -> q (i j) r"),
                     op0=ALU.mult,
                     op1=ALU.mult,
                 )
             return prod
 
         def add_pairs(prod, result_half):
-            terms = prod[:].rearrange("q r h (j i) -> q i h j r", i=2)
             nc.gpsimd.tensor_tensor(
-                out=result_half.rearrange("q (h j r) -> q h j r", h=BANK_HEADS, r=2),
-                in0=terms[:, 0],
-                in1=terms[:, 1],
+                out=result_half.rearrange("q (h f) -> q h f", h=BANK_HEADS),
+                in0=prod[:, :, 0, :],
+                in1=prod[:, :, 1, :],
                 op=ALU.add,
             )
 

@@ -30,7 +30,7 @@ X_BLOCKS = GROUPS * (GROUP // BLOCK_ROWS) * K_PASSES
 W_CHUNKS = HEADS * HEAD_DIM // BLOCK_ROWS
 BANK_HEADS = 4
 PROJECT_AHEAD = TILES
-QUANTISE_AHEAD = 2 * TILES
+QUANTISE_AHEAD = 10
 
 FLOPS = 2 * TOKENS * K * HEADS * HEAD_DIM
 
@@ -52,9 +52,8 @@ def tile_selfattention_pa_t_kernel(tc, x, freqs, w, b, g, out):
         small_pool = ctx.enter_context(tc.tile_pool(name="small_pool", bufs=4))
         prod_pool = ctx.enter_context(tc.tile_pool(name="prod_pool", bufs=4))
         result_pool = ctx.enter_context(tc.tile_pool(name="result_pool", bufs=3))
-        words_psum = ctx.enter_context(tc.psum_pool(name="words_psum", bufs=2))
         acc_psum = ctx.enter_context(tc.psum_pool(name="acc_psum", bufs=2))
-        u_psum = ctx.enter_context(tc.psum_pool(name="u_psum", bufs=4))
+        turned_psum = ctx.enter_context(tc.psum_pool(name="turned_psum", bufs=6))
         ctx.enter_context(tc.manual_schedule())
 
         x_sb = keep.tile([P, GROUPS, TILES, K], BF16, name="x_sb")
@@ -62,8 +61,8 @@ def tile_selfattention_pa_t_kernel(tc, x, freqs, w, b, g, out):
         b_rows_bf = keep.tile([HEADS, HEAD_DIM], BF16, name="b_rows_bf")
         g_all = keep.tile([P, HEAD_DIM], BF16, name="g_all")
         freqs_sb = keep.tile([P, SEQ_HALVES, TILES, 4 * PAIRS], BF16, name="freqs_sb")
-        nc.sync.dma_start(out=x_sb[:, 0], in_=x_groups[0])
         nc.sync.dma_start(out=b_rows_bf[:], in_=b.rearrange("(h d) -> h d", d=HEAD_DIM))
+        nc.sync.dma_start(out=x_sb[:, 0], in_=x_groups[0])
         nc.sync.dma_start(out=w_sb[:, 0:2, :], in_=w_chunks[0])
         nc.sync.dma_start(out=x_sb[:, 1], in_=x_groups[1])
         for c in range(1, W_CHUNKS):
@@ -80,8 +79,16 @@ def tile_selfattention_pa_t_kernel(tc, x, freqs, w, b, g, out):
             out=sort_pairs[:].rearrange("q (i j) -> q i j", i=2), in_=ident[:].rearrange("q (j i) -> q i j", i=2)
         )
 
+        b_rows = keep.tile([P, P], F32, name="b_rows")
+        nc.vector.memset(b_rows[:], 0.0)
+        nc.vector.tensor_copy(out=b_rows[0:HEADS, :], in_=b_rows_bf[:])
+        b_turned = turned_psum.tile([P, P], F32, name="b_turned", tag="turned")
+        nc.tensor.transpose(b_turned[:], b_rows[:], ident[:])
+        b_col = keep.tile([P, HEADS], F32, name="b_col")
+        nc.vector.tensor_copy(out=b_col[:], in_=b_turned[:, 0:HEADS])
+
         def transpose_block(rows, k_pass):
-            words = words_psum.tile([P, 2, BLOCK_ROWS], F32, name="words")
+            words = turned_psum.tile([P, 2, BLOCK_ROWS], F32, name="words", tag="turned")
             for u in range(2):
                 first = WORDS_PER_PASS * k_pass + P * u
                 for r in range(2):
@@ -129,24 +136,18 @@ def tile_selfattention_pa_t_kernel(tc, x, freqs, w, b, g, out):
 
         for block in range(QUANTISE_AHEAD - PROJECT_AHEAD):
             quantise_x_block(block, transpose_x_block(block))
-
-        b_rows = keep.tile([P, P], F32, name="b_rows")
-        nc.vector.memset(b_rows[:], 0.0)
-        nc.vector.tensor_copy(out=b_rows[0:HEADS, :], in_=b_rows_bf[:])
-        b_turned = words_psum.tile([P, 2, BLOCK_ROWS], F32, name="words")
-        nc.tensor.transpose(b_turned[:, 0, 0:P], b_rows[:], ident[:])
-        b_col = keep.tile([P, HEADS], F32, name="b_col")
-        nc.vector.tensor_copy(out=b_col[:], in_=b_turned[:, 0, 0:HEADS])
+        quantise_w_chunk(0)
 
         matrices = keep.tile([P, SEQ_HALVES, TILES, 2, PAIRS, 2], F32, name="matrices")
 
-        def build_matrices(e, t):
-            nc.vector.tensor_tensor(
-                out=matrices[:, e, t],
-                in0=freqs_sb[:, e, t, :].rearrange("q (j r i) -> q i j r", r=2, i=2),
-                in1=g_all[:].rearrange("q (j i) -> q i j", i=2).unsqueeze(3).to_broadcast([P, 2, PAIRS, 2]),
-                op=ALU.mult,
-            )
+        for e in range(SEQ_HALVES):
+            for t in range(TILES):
+                nc.gpsimd.tensor_tensor(
+                    out=matrices[:, e, t],
+                    in0=freqs_sb[:, e, t, :].rearrange("q (j r i) -> q i j r", r=2, i=2),
+                    in1=g_all[:].rearrange("q (j i) -> q i j", i=2).unsqueeze(3).to_broadcast([P, 2, PAIRS, 2]),
+                    op=ALU.mult,
+                )
 
         biased = {}
 
@@ -172,7 +173,7 @@ def tile_selfattention_pa_t_kernel(tc, x, freqs, w, b, g, out):
             )
 
         def turn_back(group, t, bank):
-            u = u_psum.tile([P, BANK_HEADS, HEAD_DIM], F32, name="u")
+            u = turned_psum.tile([P, BANK_HEADS, HEAD_DIM], F32, name="u", tag="turned")
             for h in range(BANK_HEADS):
                 nc.tensor.transpose(
                     u[:, h, :], biased[group, BANK_HEADS * bank + h][:, P * t : P * (t + 1)], sort_pairs[:]
@@ -224,13 +225,15 @@ def tile_selfattention_pa_t_kernel(tc, x, freqs, w, b, g, out):
             block = i + QUANTISE_AHEAD
             group, t = divmod(i, TILES)
 
+            if not finishing and head_pair + 1 < W_CHUNKS:
+                quantise_w_chunk(head_pair + 1)
             if finishing:
                 u_0 = turn_back(group, t, 0)
-                u_1 = turn_back(group, t, 1)
-            else:
-                quantise_w_chunk(head_pair)
             if projecting:
                 acc_0 = project(ahead_group, 2 * head_pair)
+            if finishing:
+                u_1 = turn_back(group, t, 1)
+            if projecting:
                 acc_1 = project(ahead_group, 2 * head_pair + 1)
             if finishing:
                 sums_0 = sum_squares(u_0)
@@ -238,16 +241,13 @@ def tile_selfattention_pa_t_kernel(tc, x, freqs, w, b, g, out):
                 add_bias(acc_0, ahead_group, 2 * head_pair)
             if finishing:
                 rstd_0 = inverse_rms(sums_0)
+                sums_1 = sum_squares(u_1)
             if projecting:
                 add_bias(acc_1, ahead_group, 2 * head_pair + 1)
-            if finishing:
-                sums_1 = sum_squares(u_1)
             if block < X_BLOCKS:
                 grouped = transpose_x_block(block)
             if finishing:
                 rstd_1 = inverse_rms(sums_1)
-                if group < SEQ_HALVES:
-                    build_matrices(group, t)
                 matrix = matrices[:, group % SEQ_HALVES, t]
                 result = result_pool.tile([P, HEADS * HEAD_DIM], F32, name="result")
                 add_pairs(multiply(u_0, rstd_0, matrix), result[:, 0:bank_cols])

@@ -50,7 +50,7 @@ def tile_selfattention_pa_t_kernel(tc, x, freqs, w, b, g, out):
         x_mx_pool = ctx.enter_context(tc.tile_pool(name="x_mx_pool", bufs=3))
         biased_pool = ctx.enter_context(tc.tile_pool(name="biased_pool", bufs=2 * HEADS))
         small_pool = ctx.enter_context(tc.tile_pool(name="small_pool", bufs=4))
-        prod_pool = ctx.enter_context(tc.tile_pool(name="prod_pool", bufs=4))
+        prod_pool = ctx.enter_context(tc.tile_pool(name="prod_pool", bufs=3))
         result_pool = ctx.enter_context(tc.tile_pool(name="result_pool", bufs=3))
         acc_psum = ctx.enter_context(tc.psum_pool(name="acc_psum", bufs=2))
         turned_psum = ctx.enter_context(tc.psum_pool(name="turned_psum", bufs=6))
@@ -62,7 +62,8 @@ def tile_selfattention_pa_t_kernel(tc, x, freqs, w, b, g, out):
         g_all = keep.tile([P, HEAD_DIM], BF16, name="g_all")
         freqs_sb = keep.tile([P, SEQ_HALVES, TILES, 4 * PAIRS], BF16, name="freqs_sb")
         nc.sync.dma_start(out=b_rows_bf[:], in_=b.rearrange("(h d) -> h d", d=HEAD_DIM))
-        nc.sync.dma_start(out=x_sb[:, 0], in_=x_groups[0])
+        nc.sync.dma_start(out=x_sb[:, 0, 0:2], in_=x_groups[0][:, 0:2])
+        nc.sync.dma_start(out=x_sb[:, 0, 2:4], in_=x_groups[0][:, 2:4])
         nc.sync.dma_start(out=w_sb[:, 0:2, :], in_=w_chunks[0])
         nc.sync.dma_start(out=x_sb[:, 1], in_=x_groups[1])
         for c in range(1, W_CHUNKS):
@@ -196,28 +197,20 @@ def tile_selfattention_pa_t_kernel(tc, x, freqs, w, b, g, out):
             )
             return rstd
 
-        def multiply(u, rstd, matrix):
-            prod = prod_pool.tile([P, BANK_HEADS, 2, HEAD_DIM], F32, name="prod")
+        def multiply(u, rstd, matrix, prod_bank):
             for h in range(BANK_HEADS):
                 nc.vector.scalar_tensor_tensor(
-                    out=prod[:, h].rearrange("q i (j r) -> q (i j) r", r=2),
+                    out=prod_bank[:, h].rearrange("q i (j r) -> q (i j) r", r=2),
                     in0=u[:, h, :].unsqueeze(2).to_broadcast([P, HEAD_DIM, 2]),
                     scalar=rstd[:, h : h + 1],
                     in1=matrix.rearrange("q i j r -> q (i j) r"),
                     op0=ALU.mult,
                     op1=ALU.mult,
                 )
-            return prod
 
-        def add_pairs(prod, result_half):
-            nc.gpsimd.tensor_tensor(
-                out=result_half.rearrange("q (h f) -> q h f", h=BANK_HEADS),
-                in0=prod[:, :, 0, :],
-                in1=prod[:, :, 1, :],
-                op=ALU.add,
-            )
+        def add_pairs(prod, result):
+            nc.gpsimd.tensor_tensor(out=result[:], in0=prod[:, :, 0, :], in1=prod[:, :, 1, :], op=ALU.add)
 
-        bank_cols = BANK_HEADS * HEAD_DIM
         for i in range(-PROJECT_AHEAD, ALL_TILES):
             ahead_group, head_pair = divmod(i + PROJECT_AHEAD, TILES)
             projecting = ahead_group < GROUPS
@@ -249,10 +242,12 @@ def tile_selfattention_pa_t_kernel(tc, x, freqs, w, b, g, out):
             if finishing:
                 rstd_1 = inverse_rms(sums_1)
                 matrix = matrices[:, group % SEQ_HALVES, t]
-                result = result_pool.tile([P, HEADS * HEAD_DIM], F32, name="result")
-                add_pairs(multiply(u_0, rstd_0, matrix), result[:, 0:bank_cols])
+                prod = prod_pool.tile([P, HEADS, 2, HEAD_DIM], F32, name="prod")
+                multiply(u_0, rstd_0, matrix, prod[:, 0:BANK_HEADS])
             if block < X_BLOCKS:
                 quantise_x_block(block, grouped)
             if finishing:
-                add_pairs(multiply(u_1, rstd_1, matrix), result[:, bank_cols : 2 * bank_cols])
-                nc.sync.dma_start(out=out_tiles[group, t], in_=result[:])
+                multiply(u_1, rstd_1, matrix, prod[:, BANK_HEADS:HEADS])
+                result = result_pool.tile([P, HEADS, HEAD_DIM], F32, name="result")
+                add_pairs(prod, result)
+                nc.sync.dma_start(out=out_tiles[group, t], in_=result[:].rearrange("q h f -> q (h f)"))

@@ -26,7 +26,8 @@ TILES = GROUP // P
 ALL_TILES = GROUPS * TILES
 SEQ_HALVES = 2
 BLOCK_ROWS = 256
-X_BLOCKS = GROUPS * (GROUP // BLOCK_ROWS) * K_PASSES
+BLOCKS_PER_GROUP = (GROUP // BLOCK_ROWS) * K_PASSES
+X_BLOCKS = GROUPS * BLOCKS_PER_GROUP
 W_CHUNKS = HEADS * HEAD_DIM // BLOCK_ROWS
 BANK_HEADS = 4
 PROJECT_AHEAD = TILES
@@ -46,11 +47,12 @@ def tile_selfattention_pa_t_kernel(tc, x, freqs, w, b, g, out):
 
     with ExitStack() as ctx:
         keep = ctx.enter_context(tc.tile_pool(name="keep", bufs=1))
-        grouped_pool = ctx.enter_context(tc.tile_pool(name="grouped_pool", bufs=3))
+        x_grouped_pool = ctx.enter_context(tc.tile_pool(name="x_grouped_pool", bufs=2))
+        w_grouped_pool = ctx.enter_context(tc.tile_pool(name="w_grouped_pool", bufs=2))
         x_mx_pool = ctx.enter_context(tc.tile_pool(name="x_mx_pool", bufs=3))
         biased_pool = ctx.enter_context(tc.tile_pool(name="biased_pool", bufs=2 * HEADS))
         small_pool = ctx.enter_context(tc.tile_pool(name="small_pool", bufs=4))
-        prod_pool = ctx.enter_context(tc.tile_pool(name="prod_pool", bufs=3))
+        prod_pool = ctx.enter_context(tc.tile_pool(name="prod_pool", bufs=4))
         result_pool = ctx.enter_context(tc.tile_pool(name="result_pool", bufs=3))
         acc_psum = ctx.enter_context(tc.psum_pool(name="acc_psum", bufs=2))
         turned_psum = ctx.enter_context(tc.psum_pool(name="turned_psum", bufs=6))
@@ -62,8 +64,7 @@ def tile_selfattention_pa_t_kernel(tc, x, freqs, w, b, g, out):
         g_all = keep.tile([P, HEAD_DIM], BF16, name="g_all")
         freqs_sb = keep.tile([P, SEQ_HALVES, TILES, 4 * PAIRS], BF16, name="freqs_sb")
         nc.sync.dma_start(out=b_rows_bf[:], in_=b.rearrange("(h d) -> h d", d=HEAD_DIM))
-        nc.sync.dma_start(out=x_sb[:, 0, 0:2], in_=x_groups[0][:, 0:2])
-        nc.sync.dma_start(out=x_sb[:, 0, 2:4], in_=x_groups[0][:, 2:4])
+        nc.sync.dma_start(out=x_sb[:, 0], in_=x_groups[0])
         nc.sync.dma_start(out=w_sb[:, 0:2, :], in_=w_chunks[0])
         nc.sync.dma_start(out=x_sb[:, 1], in_=x_groups[1])
         for c in range(1, W_CHUNKS):
@@ -88,7 +89,7 @@ def tile_selfattention_pa_t_kernel(tc, x, freqs, w, b, g, out):
         b_col = keep.tile([P, HEADS], F32, name="b_col")
         nc.vector.tensor_copy(out=b_col[:], in_=b_turned[:, 0:HEADS])
 
-        def transpose_block(rows, k_pass):
+        def transpose_block(rows, k_pass, grouped):
             words = turned_psum.tile([P, 2, BLOCK_ROWS], F32, name="words", tag="turned")
             for u in range(2):
                 first = WORDS_PER_PASS * k_pass + P * u
@@ -98,45 +99,51 @@ def tile_selfattention_pa_t_kernel(tc, x, freqs, w, b, g, out):
                         rows[:, r, :].bitcast(F32)[:, first : first + P],
                         ident[:],
                     )
-            grouped = grouped_pool.tile([P, 4 * BLOCK_ROWS], BF16, name="grouped", align_bytes=64)
             copy_out = nc.scalar.copy if k_pass == 0 else nc.vector.tensor_copy
             copy_out(
-                out=grouped[:].bitcast(F32).rearrange("q (n u) -> q n u", u=2),
+                out=grouped.bitcast(F32).rearrange("q (n u) -> q n u", u=2),
                 in_=words[:].rearrange("q u n -> q n u"),
             )
-            return grouped
 
-        def quantise_block(grouped, codes, scales):
-            nc.vector.quantize_mx(out=codes.bitcast(FP8X4), scales=scales, in_=grouped[:])
-
+        x_grouped = {}
         x_codes = {}
         x_scales = {}
 
-        def transpose_x_block(block):
-            group, rest = divmod(block, X_BLOCKS // GROUPS)
+        def prepare_x_block(block):
+            group, rest = divmod(block, BLOCKS_PER_GROUP)
             half, k_pass = divmod(rest, K_PASSES)
             if rest == 0:
+                x_grouped[group] = x_grouped_pool.tile(
+                    [P, K_PASSES, GROUP // BLOCK_ROWS, 4 * BLOCK_ROWS], BF16, name="x_grouped", align_bytes=64
+                )
                 x_codes[group] = x_mx_pool.tile([P, K_PASSES, GROUP], U32, name="x_codes", align_bytes=64)
                 x_scales[group] = x_mx_pool.tile([P, K_PASSES, GROUP], U8, name="x_scales", align_bytes=64)
-            return transpose_block(x_sb[:, group, 2 * half : 2 * half + 2, :], k_pass)
+            transpose_block(x_sb[:, group, 2 * half : 2 * half + 2, :], k_pass, x_grouped[group][:, k_pass, half, :])
 
-        def quantise_x_block(block, grouped):
-            group, rest = divmod(block, X_BLOCKS // GROUPS)
-            half, k_pass = divmod(rest, K_PASSES)
-            cols = slice(BLOCK_ROWS * half, BLOCK_ROWS * (half + 1))
-            quantise_block(grouped, x_codes[group][:, k_pass, cols], x_scales[group][:, k_pass, cols])
+        def quantise_x_group(group):
+            nc.vector.quantize_mx(
+                out=x_codes[group][:].rearrange("q c n -> q (c n)").bitcast(FP8X4),
+                scales=x_scales[group][:].rearrange("q c n -> q (c n)"),
+                in_=x_grouped[group][:].rearrange("q c e n -> q (c e n)"),
+            )
 
-        w_codes = keep.tile([P, K_PASSES, HEADS * HEAD_DIM], U32, name="w_codes", align_bytes=64)
-        w_scales = keep.tile([P, K_PASSES, HEADS * HEAD_DIM], U8, name="w_scales", align_bytes=64)
+        w_codes = keep.tile([P, W_CHUNKS, K_PASSES, BLOCK_ROWS], U32, name="w_codes", align_bytes=64)
+        w_scales = keep.tile([P, W_CHUNKS, K_PASSES, BLOCK_ROWS], U8, name="w_scales", align_bytes=64)
 
         def quantise_w_chunk(c):
-            cols = slice(BLOCK_ROWS * c, BLOCK_ROWS * (c + 1))
+            w_grouped = w_grouped_pool.tile([P, K_PASSES, 4 * BLOCK_ROWS], BF16, name="w_grouped", align_bytes=64)
             for k_pass in range(K_PASSES):
-                grouped = transpose_block(w_sb[:, 2 * c : 2 * c + 2, :], k_pass)
-                quantise_block(grouped, w_codes[:, k_pass, cols], w_scales[:, k_pass, cols])
+                transpose_block(w_sb[:, 2 * c : 2 * c + 2, :], k_pass, w_grouped[:, k_pass, :])
+            nc.vector.quantize_mx(
+                out=w_codes[:, c].rearrange("q c n -> q (c n)").bitcast(FP8X4),
+                scales=w_scales[:, c].rearrange("q c n -> q (c n)"),
+                in_=w_grouped[:].rearrange("q c n -> q (c n)"),
+            )
 
         for block in range(QUANTISE_AHEAD - PROJECT_AHEAD):
-            quantise_x_block(block, transpose_x_block(block))
+            prepare_x_block(block)
+            if block == BLOCKS_PER_GROUP - 1:
+                quantise_x_group(0)
         quantise_w_chunk(0)
 
         matrices = keep.tile([P, SEQ_HALVES, TILES, 2, PAIRS, 2], F32, name="matrices")
@@ -154,12 +161,13 @@ def tile_selfattention_pa_t_kernel(tc, x, freqs, w, b, g, out):
 
         def project(group, head):
             acc = acc_psum.tile([P, GROUP], F32, name="acc")
-            feats = slice(HEAD_DIM * head, HEAD_DIM * (head + 1))
+            chunk, place = divmod(head, 2)
+            feats = slice(HEAD_DIM * place, HEAD_DIM * (place + 1))
             for k_pass in range(K_PASSES):
                 nc.tensor.matmul_mx(
                     out=acc[:],
-                    lhsT=w_codes[:, k_pass, feats].bitcast(FP8X4),
-                    lhsT_scale=w_scales[:, k_pass, feats],
+                    lhsT=w_codes[:, chunk, k_pass, feats].bitcast(FP8X4),
+                    lhsT_scale=w_scales[:, chunk, k_pass, feats],
                     rhs=x_codes[group][:, k_pass, :].bitcast(FP8X4),
                     rhs_scale=x_scales[group][:, k_pass, :],
                     start=(k_pass == 0),
@@ -197,20 +205,28 @@ def tile_selfattention_pa_t_kernel(tc, x, freqs, w, b, g, out):
             )
             return rstd
 
-        def multiply(u, rstd, matrix, prod_bank):
+        def multiply(u, rstd, matrix):
+            prod = prod_pool.tile([P, BANK_HEADS, 2, HEAD_DIM], F32, name="prod")
             for h in range(BANK_HEADS):
                 nc.vector.scalar_tensor_tensor(
-                    out=prod_bank[:, h].rearrange("q i (j r) -> q (i j) r", r=2),
+                    out=prod[:, h].rearrange("q i (j r) -> q (i j) r", r=2),
                     in0=u[:, h, :].unsqueeze(2).to_broadcast([P, HEAD_DIM, 2]),
                     scalar=rstd[:, h : h + 1],
                     in1=matrix.rearrange("q i j r -> q (i j) r"),
                     op0=ALU.mult,
                     op1=ALU.mult,
                 )
+            return prod
 
-        def add_pairs(prod, result):
-            nc.gpsimd.tensor_tensor(out=result[:], in0=prod[:, :, 0, :], in1=prod[:, :, 1, :], op=ALU.add)
+        def add_pairs(prod, result_half):
+            nc.gpsimd.tensor_tensor(
+                out=result_half.rearrange("q (h f) -> q h f", h=BANK_HEADS),
+                in0=prod[:, :, 0, :],
+                in1=prod[:, :, 1, :],
+                op=ALU.add,
+            )
 
+        bank_cols = BANK_HEADS * HEAD_DIM
         for i in range(-PROJECT_AHEAD, ALL_TILES):
             ahead_group, head_pair = divmod(i + PROJECT_AHEAD, TILES)
             projecting = ahead_group < GROUPS
@@ -238,16 +254,14 @@ def tile_selfattention_pa_t_kernel(tc, x, freqs, w, b, g, out):
             if projecting:
                 add_bias(acc_1, ahead_group, 2 * head_pair + 1)
             if block < X_BLOCKS:
-                grouped = transpose_x_block(block)
+                prepare_x_block(block)
             if finishing:
                 rstd_1 = inverse_rms(sums_1)
                 matrix = matrices[:, group % SEQ_HALVES, t]
-                prod = prod_pool.tile([P, HEADS, 2, HEAD_DIM], F32, name="prod")
-                multiply(u_0, rstd_0, matrix, prod[:, 0:BANK_HEADS])
-            if block < X_BLOCKS:
-                quantise_x_block(block, grouped)
+                result = result_pool.tile([P, HEADS * HEAD_DIM], F32, name="result")
+                add_pairs(multiply(u_0, rstd_0, matrix), result[:, 0:bank_cols])
+            if block < X_BLOCKS and block % BLOCKS_PER_GROUP == BLOCKS_PER_GROUP - 1:
+                quantise_x_group(block // BLOCKS_PER_GROUP)
             if finishing:
-                multiply(u_1, rstd_1, matrix, prod[:, BANK_HEADS:HEADS])
-                result = result_pool.tile([P, HEADS, HEAD_DIM], F32, name="result")
-                add_pairs(prod, result)
-                nc.sync.dma_start(out=out_tiles[group, t], in_=result[:].rearrange("q h f -> q (h f)"))
+                add_pairs(multiply(u_1, rstd_1, matrix), result[:, bank_cols : 2 * bank_cols])
+                nc.sync.dma_start(out=out_tiles[group, t], in_=result[:])

@@ -64,7 +64,8 @@ def tile_selfattention_pa_t_kernel(tc, x, freqs, w, b, g, out):
         g_all = keep.tile([P, HEAD_DIM], BF16, name="g_all")
         freqs_sb = keep.tile([P, SEQ_HALVES, TILES, 4 * PAIRS], BF16, name="freqs_sb")
         nc.sync.dma_start(out=b_rows_bf[:], in_=b.rearrange("(h d) -> h d", d=HEAD_DIM))
-        nc.sync.dma_start(out=x_sb[:, 0], in_=x_groups[0])
+        nc.sync.dma_start(out=x_sb[:, 0, 0:2], in_=x_groups[0][:, 0:2])
+        nc.sync.dma_start(out=x_sb[:, 0, 2:4], in_=x_groups[0][:, 2:4])
         nc.sync.dma_start(out=w_sb[:, 0:2, :], in_=w_chunks[0])
         nc.sync.dma_start(out=x_sb[:, 1], in_=x_groups[1])
         for c in range(1, W_CHUNKS):

from contextlib import ExitStack

import concourse.mybir as mybir
from concourse.masks import make_identity

F32 = mybir.dt.float32
BF16 = mybir.dt.bfloat16
U32 = mybir.dt.uint32
U8 = mybir.dt.uint8
FP8X4 = mybir.dt.float8_e4m3fn_x4
ACT = mybir.ActivationFunctionType
ALU = mybir.AluOpType

P = 128
K = 1024
K_PASSES = 2
WORDS_PER_PASS = 256
HEADS = 8
HEAD_DIM = 128
PAIRS = HEAD_DIM // 2
EPS = 1e-6
TOKENS = 4096
GROUP = 512
GROUPS = TOKENS // GROUP
TILES = GROUP // P
ALL_TILES = GROUPS * TILES
SEQ_HALVES = 2
BLOCK_ROWS = 256
BLOCKS_PER_GROUP = (GROUP // BLOCK_ROWS) * K_PASSES
X_BLOCKS = GROUPS * BLOCKS_PER_GROUP
W_CHUNKS = HEADS * HEAD_DIM // BLOCK_ROWS
BANK_HEADS = 4
PROJECT_AHEAD = TILES
QUANTISE_AHEAD = 10

FLOPS = 2 * TOKENS * K * HEADS * HEAD_DIM


def tile_selfattention_pa_t_kernel(tc, x, freqs, w, b, g, out):
    nc = tc.nc
    x_groups = x.rearrange("n s k -> (n s) k").rearrange("(a q t) k -> a q t k", q=P, t=TILES)
    out_tiles = out.rearrange("n s h d -> (n s) (h d)").rearrange("(a q t) f -> a t q f", q=P, t=TILES)
    w_chunks = w.rearrange("(c r q) k -> c q r k", r=2, q=P)
    freqs_rows = freqs.rearrange("a s b j r i -> (a s b) (j r i)").rearrange(
        "(e q t) f -> q e t f", q=P, t=TILES
    )

    with ExitStack() as ctx:
        keep = ctx.enter_context(tc.tile_pool(name="keep", bufs=1))
        x_grouped_pool = ctx.enter_context(tc.tile_pool(name="x_grouped_pool", bufs=2))
        w_grouped_pool = ctx.enter_context(tc.tile_pool(name="w_grouped_pool", bufs=2))
        x_mx_pool = ctx.enter_context(tc.tile_pool(name="x_mx_pool", bufs=3))
        biased_pool = ctx.enter_context(tc.tile_pool(name="biased_pool", bufs=2 * HEADS))
        small_pool = ctx.enter_context(tc.tile_pool(name="small_pool", bufs=4))
        prod_pool = ctx.enter_context(tc.tile_pool(name="prod_pool", bufs=4))
        result_pool = ctx.enter_context(tc.tile_pool(name="result_pool", bufs=3))
        acc_psum = ctx.enter_context(tc.psum_pool(name="acc_psum", bufs=2))
        turned_psum = ctx.enter_context(tc.psum_pool(name="turned_psum", bufs=6))
        ctx.enter_context(tc.manual_schedule())

        x_sb = keep.tile([P, GROUPS, TILES, K], BF16, name="x_sb")
        w_sb = keep.tile([P, HEADS, K], BF16, name="w_sb")
        b_rows_bf = keep.tile([HEADS, HEAD_DIM], BF16, name="b_rows_bf")
        g_all = keep.tile([P, HEAD_DIM], BF16, name="g_all")
        freqs_sb = keep.tile([P, SEQ_HALVES, TILES, 4 * PAIRS], BF16, name="freqs_sb")
        nc.sync.dma_start(out=b_rows_bf[:], in_=b.rearrange("(h d) -> h d", d=HEAD_DIM))
        nc.sync.dma_start(out=x_sb[:, 0, 0:2], in_=x_groups[0][:, 0:2])
        nc.sync.dma_start(out=x_sb[:, 0, 2:4], in_=x_groups[0][:, 2:4])
        nc.sync.dma_start(out=w_sb[:, 0:2, :], in_=w_chunks[0])
        nc.sync.dma_start(out=x_sb[:, 1], in_=x_groups[1])
        for c in range(1, W_CHUNKS):
            nc.sync.dma_start(out=w_sb[:, 2 * c : 2 * c + 2, :], in_=w_chunks[c])
        nc.sync.dma_start(out=g_all[:], in_=g.partition_broadcast(P))
        nc.sync.dma_start(out=freqs_sb[:], in_=freqs_rows)
        for a in range(2, GROUPS):
            nc.sync.dma_start(out=x_sb[:, a], in_=x_groups[a])

        ident = keep.tile([P, P], F32, name="ident")
        make_identity(nc, ident[:])
        sort_pairs = keep.tile([P, P], F32, name="sort_pairs")
        nc.vector.tensor_copy(
            out=sort_pairs[:].rearrange("q (i j) -> q i j", i=2), in_=ident[:].rearrange("q (j i) -> q i j", i=2)
        )

        b_rows = keep.tile([P, P], F32, name="b_rows")
        nc.vector.memset(b_rows[:], 0.0)
        nc.vector.tensor_copy(out=b_rows[0:HEADS, :], in_=b_rows_bf[:])
        b_turned = turned_psum.tile([P, P], F32, name="b_turned", tag="turned")
        nc.tensor.transpose(b_turned[:], b_rows[:], ident[:])
        b_col = keep.tile([P, HEADS], F32, name="b_col")
        nc.vector.tensor_copy(out=b_col[:], in_=b_turned[:, 0:HEADS])

        def transpose_block(rows, k_pass, grouped):
            words = turned_psum.tile([P, 2, BLOCK_ROWS], F32, name="words", tag="turned")
            for u in range(2):
                first = WORDS_PER_PASS * k_pass + P * u
                for r in range(2):
                    nc.tensor.transpose(
                        words[:, u, P * r : P * (r + 1)],
                        rows[:, r, :].bitcast(F32)[:, first : first + P],
                        ident[:],
                    )
            copy_out = nc.scalar.copy if k_pass == 0 else nc.vector.tensor_copy
            copy_out(
                out=grouped.bitcast(F32).rearrange("q (n u) -> q n u", u=2),
                in_=words[:].rearrange("q u n -> q n u"),
            )

        x_grouped = {}
        x_codes = {}
        x_scales = {}

        def prepare_x_block(block):
            group, rest = divmod(block, BLOCKS_PER_GROUP)
            half, k_pass = divmod(rest, K_PASSES)
            if rest == 0:
                x_grouped[group] = x_grouped_pool.tile(
                    [P, K_PASSES, GROUP // BLOCK_ROWS, 4 * BLOCK_ROWS], BF16, name="x_grouped", align_bytes=64
                )
                x_codes[group] = x_mx_pool.tile([P, K_PASSES, GROUP], U32, name="x_codes", align_bytes=64)
                x_scales[group] = x_mx_pool.tile([P, K_PASSES, GROUP], U8, name="x_scales", align_bytes=64)
            transpose_block(x_sb[:, group, 2 * half : 2 * half + 2, :], k_pass, x_grouped[group][:, k_pass, half, :])

        def quantise_x_group(group):
            nc.vector.quantize_mx(
                out=x_codes[group][:].rearrange("q c n -> q (c n)").bitcast(FP8X4),
                scales=x_scales[group][:].rearrange("q c n -> q (c n)"),
                in_=x_grouped[group][:].rearrange("q c e n -> q (c e n)"),
            )

        w_codes = keep.tile([P, W_CHUNKS, K_PASSES, BLOCK_ROWS], U32, name="w_codes", align_bytes=64)
        w_scales = keep.tile([P, W_CHUNKS, K_PASSES, BLOCK_ROWS], U8, name="w_scales", align_bytes=64)

        def quantise_w_chunk(c):
            w_grouped = w_grouped_pool.tile([P, K_PASSES, 4 * BLOCK_ROWS], BF16, name="w_grouped", align_bytes=64)
            for k_pass in range(K_PASSES):
                transpose_block(w_sb[:, 2 * c : 2 * c + 2, :], k_pass, w_grouped[:, k_pass, :])
            nc.vector.quantize_mx(
                out=w_codes[:, c].rearrange("q c n -> q (c n)").bitcast(FP8X4),
                scales=w_scales[:, c].rearrange("q c n -> q (c n)"),
                in_=w_grouped[:].rearrange("q c n -> q (c n)"),
            )

        for block in range(QUANTISE_AHEAD - PROJECT_AHEAD):
            prepare_x_block(block)
            if block == BLOCKS_PER_GROUP - 1:
                quantise_x_group(0)
        quantise_w_chunk(0)

        matrices = keep.tile([P, SEQ_HALVES, TILES, 2, PAIRS, 2], F32, name="matrices")

        for e in range(SEQ_HALVES):
            for t in range(TILES):
                nc.gpsimd.tensor_tensor(
                    out=matrices[:, e, t],
                    in0=freqs_sb[:, e, t, :].rearrange("q (j r i) -> q i j r", r=2, i=2),
                    in1=g_all[:].rearrange("q (j i) -> q i j", i=2).unsqueeze(3).to_broadcast([P, 2, PAIRS, 2]),
                    op=ALU.mult,
                )

        biased = {}

        def project(group, head):
            acc = acc_psum.tile([P, GROUP], F32, name="acc")
            chunk, place = divmod(head, 2)
            feats = slice(HEAD_DIM * place, HEAD_DIM * (place + 1))
            for k_pass in range(K_PASSES):
                nc.tensor.matmul_mx(
                    out=acc[:],
                    lhsT=w_codes[:, chunk, k_pass, feats].bitcast(FP8X4),
                    lhsT_scale=w_scales[:, chunk, k_pass, feats],
                    rhs=x_codes[group][:, k_pass, :].bitcast(FP8X4),
                    rhs_scale=x_scales[group][:, k_pass, :],
                    start=(k_pass == 0),
                    stop=(k_pass == K_PASSES - 1),
                )
            return acc

        def add_bias(acc, group, head):
            biased[group, head] = biased_pool.tile([P, GROUP], F32, name="biased")
            nc.scalar.activation(
                out=biased[group, head][:], in_=acc[:], func=ACT.Identity, bias=b_col[:, head : head + 1], scale=1.0
            )

        def turn_back(group, t, bank):
            u = turned_psum.tile([P, BANK_HEADS, HEAD_DIM], F32, name="u", tag="turned")
            for h in range(BANK_HEADS):
                nc.tensor.transpose(
                    u[:, h, :], biased[group, BANK_HEADS * bank + h][:, P * t : P * (t + 1)], sort_pairs[:]
                )
            return u

        def sum_squares(u):
            sums = small_pool.tile([P, BANK_HEADS], F32, name="sums")
            squares = small_pool.tile([P, BANK_HEADS, HEAD_DIM], F32, name="squares")
            for h in range(BANK_HEADS):
                nc.scalar.activation(
                    out=squares[:, h, :], in_=u[:, h, :], func=ACT.Square, accum_out=sums[:, h : h + 1]
                )
            return sums

        def inverse_rms(sums):
            rstd = small_pool.tile([P, BANK_HEADS], F32, name="rstd")
            nc.scalar.activation(
                out=rstd[:], in_=sums[:], func=ACT.Abs_reciprocal_sqrt, scale=1.0 / HEAD_DIM, bias=EPS
            )
            return rstd

        def multiply(u, rstd, matrix):
            prod = prod_pool.tile([P, BANK_HEADS, 2, HEAD_DIM], F32, name="prod")
            for h in range(BANK_HEADS):
                nc.vector.scalar_tensor_tensor(
                    out=prod[:, h].rearrange("q i (j r) -> q (i j) r", r=2),
                    in0=u[:, h, :].unsqueeze(2).to_broadcast([P, HEAD_DIM, 2]),
                    scalar=rstd[:, h : h + 1],
                    in1=matrix.rearrange("q i j r -> q (i j) r"),
                    op0=ALU.mult,
                    op1=ALU.mult,
                )
            return prod

        def add_pairs(prod, result_half):
            nc.gpsimd.tensor_tensor(
                out=result_half.rearrange("q (h f) -> q h f", h=BANK_HEADS),
                in0=prod[:, :, 0, :],
                in1=prod[:, :, 1, :],
                op=ALU.add,
            )

        bank_cols = BANK_HEADS * HEAD_DIM
        for i in range(-PROJECT_AHEAD, ALL_TILES):
            ahead_group, head_pair = divmod(i + PROJECT_AHEAD, TILES)
            projecting = ahead_group < GROUPS
            finishing = i >= 0
            block = i + QUANTISE_AHEAD
            group, t = divmod(i, TILES)

            if not finishing and head_pair + 1 < W_CHUNKS:
                quantise_w_chunk(head_pair + 1)
            if finishing:
                u_0 = turn_back(group, t, 0)
            if projecting:
                acc_0 = project(ahead_group, 2 * head_pair)
            if finishing:
                u_1 = turn_back(group, t, 1)
            if projecting:
                acc_1 = project(ahead_group, 2 * head_pair + 1)
            if finishing:
                sums_0 = sum_squares(u_0)
            if projecting:
                add_bias(acc_0, ahead_group, 2 * head_pair)
            if finishing:
                rstd_0 = inverse_rms(sums_0)
                sums_1 = sum_squares(u_1)
            if projecting:
                add_bias(acc_1, ahead_group, 2 * head_pair + 1)
            if block < X_BLOCKS:
                prepare_x_block(block)
            if finishing:
                rstd_1 = inverse_rms(sums_1)
                matrix = matrices[:, group % SEQ_HALVES, t]
                result = result_pool.tile([P, HEADS * HEAD_DIM], F32, name="result")
                add_pairs(multiply(u_0, rstd_0, matrix), result[:, 0:bank_cols])
            if block < X_BLOCKS and block % BLOCKS_PER_GROUP == BLOCKS_PER_GROUP - 1:
                quantise_x_group(block // BLOCKS_PER_GROUP)
            if finishing:
                add_pairs(multiply(u_1, rstd_1, matrix), result[:, bank_cols : 2 * bank_cols])
                nc.sync.dma_start(out=out_tiles[group, t], in_=result[:])
